import numpy as np
import ml_dtypes


def mxq(x, axis, fmt="e4m3"):
    dtype, down = {"e4m3": (ml_dtypes.float8_e4m3fn, 7), "e5m2": (ml_dtypes.float8_e5m2, 14)}[fmt]
    v = np.moveaxis(np.asarray(x, np.float32).astype(ml_dtypes.bfloat16).astype(np.float64), axis, -1)
    blocks = v.reshape(v.shape[:-1] + (-1, 32))
    amax = np.abs(blocks).max(-1, keepdims=True)
    byte = np.maximum(np.where(amax > 0, np.frexp(amax)[1] - 1 + 127, 0) - down, 1)
    scale = np.exp2(byte - 127.0)
    codes = (blocks / scale).astype(np.float32).astype(dtype).astype(np.float64)
    return np.moveaxis((codes * scale).reshape(v.shape), -1, axis)


WIDE = False


def mx_kscale(k):
    if not WIDE:
        return np.ones(k)
    levels = np.array([10, -10, 5, -5, 0])
    a = np.random.permutation(np.resize(levels, k // 512 * 4)).reshape(k // 512, 4)
    idx = np.arange(k)
    return np.exp2(a[idx // 512, idx % 128 // 32])


BF16 = ml_dtypes.bfloat16


def bf(x):
    return np.asarray(x, np.float32).astype(BF16)


def f64(x):
    return np.asarray(x).astype(np.float64)


B, S, E, HID, H = 2, 4096, 512, 1024, 8
DH = HID // H


def setup_inputs():
    t = mx_kscale(HID)
    kv_rms = np.hypot(6.0 * np.sqrt(S), 0.19 * S)
    return {"q_feat": bf(1.0 + 2.8 * np.random.standard_normal((B, H, S, DH))),
            "kv": bf(np.random.standard_normal((B, H, DH, DH)) * kv_rms * t.reshape(H, 1, DH)),
            "denom": bf(S * DH * (1.0 + 0.1 * np.random.standard_normal((B, H, 1, 1)))),
            "Wo": bf(np.random.standard_normal((HID, E)) * 4.0 / np.sqrt(HID) / t[:, None]),
            "bo": bf(np.random.standard_normal(E) * 0.1)}


def reference(q_feat, kv, denom, Wo, bo):
    qkv = f64(q_feat) @ f64(kv)
    ctx = qkv / f64(denom)
    ctx = ctx.transpose(0, 2, 1, 3).reshape(B, S, HID)
    return (mxq(ctx, 2, "e4m3") @ mxq(f64(Wo), 0, "e4m3")) + f64(bo)

@@ -1,0 +1,192 @@
+from contextlib import ExitStack
+
+import concourse.masks as masks
+import concourse.mybir as mybir
+
+BF16 = mybir.dt.bfloat16
+F32 = mybir.dt.float32
+U32 = mybir.dt.uint32
+U8 = mybir.dt.uint8
+FP8X4 = mybir.dt.float8_e4m3fn_x4
+
+P = 128
+B, H, S, DH, E = 2, 8, 4096, 128, 512
+PACK = 4
+PASSES = H // PACK
+J = 8
+CHUNK = P * J
+CHUNKS_PER_SEQ = S // CHUNK
+N_CHUNKS = B * CHUNKS_PER_SEQ
+R = 2
+N_ROUNDS = N_CHUNKS * J // R
+STORE_J = 2
+LOADS_AHEAD = 4
+
+FLOPS = 2 * B * H * S * DH * DH + 2 * B * S * H * DH * E
+
+
+def tile_linearattention_pb_t_kernel(tc, q_feat, kv, denom, Wo, bo, out):
+    nc = tc.nc
+    with ExitStack() as stack:
+        const = stack.enter_context(tc.tile_pool(name="const", bufs=1))
+        q_pool = stack.enter_context(tc.tile_pool(name="q", bufs=N_CHUNKS))
+        work = stack.enter_context(tc.tile_pool(name="work", bufs=2))
+        out_pool = stack.enter_context(tc.tile_pool(name="outs", bufs=6))
+        qT_banks = stack.enter_context(tc.psum_pool(name="qT_banks", bufs=R))
+        ctx_banks = stack.enter_context(tc.psum_pool(name="ctx_banks", bufs=R * PASSES))
+        out_banks = stack.enter_context(tc.psum_pool(name="out_banks", bufs=R))
+        stack.enter_context(tc.manual_schedule())
+
+        def load_chunk(c):
+            b, part = divmod(c, CHUNKS_PER_SEQ)
+            q_sb = q_pool.tile([P, H, J * DH], BF16, name="q_sb", tag="q_sb")
+            rows = q_feat[b, :, part * CHUNK : (part + 1) * CHUNK, :]
+            nc.sync.dma_start(out=q_sb[:], in_=rows.rearrange("h (p j) d -> p h (j d)", j=J))
+            return q_sb
+
+        bias_row = const.tile([P, E], BF16)
+        nc.vector.memset(bias_row[:], 0.0)
+        denom_bc = const.tile([P, B * H], BF16)
+        nc.sync.dma_start(out=denom_bc[:], in_=denom.rearrange("b h x y -> (b h x y)").partition_broadcast(P))
+        wo_raw = const.tile([P, H, E], BF16)
+        nc.sync.dma_start(out=wo_raw[:], in_=Wo.rearrange("(c p) n -> p c n", p=P))
+        kv_sb = const.tile([P, B, H, DH], BF16)
+        nc.sync.dma_start(out=kv_sb[:, 0], in_=kv[0].rearrange("h d e -> d h e"))
+        nc.sync.dma_start(out=bias_row[0:1, :], in_=bo.rearrange("(o n) -> o n", o=1))
+        q_tiles = {}
+        for c in range(LOADS_AHEAD):
+            q_tiles[c] = load_chunk(c)
+        nc.sync.dma_start(out=kv_sb[:, 1], in_=kv[1].rearrange("h d e -> d h e"))
+
+        identity = const.tile([P, P], BF16)
+        masks.make_identity(nc, identity[:])
+        ones = const.tile([P, P], BF16)
+        nc.vector.memset(ones[:], 1.0)
+        rden = const.tile([P, B * H], F32)
+        nc.vector.reciprocal(out=rden[:], in_=denom_bc[:])
+
+        wo_grouped = const.tile([P, PASSES, E, PACK], BF16, align_bytes=64)
+        for g in range(PASSES):
+            nc.vector.tensor_copy(
+                out=wo_grouped[:, g],
+                in_=wo_raw[:, g * PACK : (g + 1) * PACK, :].rearrange("p t n -> p n t"),
+            )
+        wo_codes = const.tile([P, PASSES, E], U32, align_bytes=64)
+        wo_scales = const.tile([P, PASSES, E], U8, align_bytes=64)
+        nc.vector.quantize_mx(
+            out=wo_codes[:].rearrange("p g n -> p (g n)").bitcast(FP8X4),
+            scales=wo_scales[:].rearrange("p g n -> p (g n)"),
+            in_=wo_grouped[:].rearrange("p g n t -> p (g n t)"),
+        )
+
+        bias_ps = out_banks.tile([P, E], F32, name="bias_ps", tag="out_ps")
+        nc.tensor.matmul(out=bias_ps[:], lhsT=ones[:], rhs=bias_row[:], start=True, stop=True)
+        bias_sb = const.tile([P, E], F32)
+        nc.vector.tensor_copy(out=bias_sb[:], in_=bias_ps[:])
+
+        qT_ps, qT_sb, ctx_ps, codes, scales, out_ps, out_sb = {}, {}, {}, {}, {}, {}, {}
+
+        def place(r, i):
+            return divmod(r * R + i, J)
+
+        def transpose_head(r, u):
+            i, h = divmod(u, H)
+            c, j = place(r, i)
+            nc.tensor.transpose(qT_ps[r][i][:, h, :], q_tiles[c][:, h, j * DH : (j + 1) * DH], identity[:])
+
+        def multiply_head(r, u):
+            i, h = divmod(u, H)
+            g, t = divmod(h, PACK)
+            b = place(r, i)[0] // CHUNKS_PER_SEQ
+            nc.tensor.matmul(
+                out=ctx_ps[r][i][g][:, t, :],
+                lhsT=kv_sb[:, b, h, :],
+                rhs=qT_sb[r][:, i, h, :],
+                start=True,
+                stop=True,
+            )
+
+        def transposes_and_first_matmul(r_t, r_m):
+            do_t = r_t < N_ROUNDS
+            do_m = 0 <= r_m < N_ROUNDS
+            if do_t:
+                qT_ps[r_t] = [qT_banks.tile([P, H, P], BF16, name="qT_ps", tag="qT_ps") for i in range(R)]
+            if do_m:
+                ctx_ps[r_m] = [
+                    [ctx_banks.tile([P, PACK, P], F32, name="ctx_ps", tag="ctx_ps") for g in range(PASSES)]
+                    for i in range(R)
+                ]
+            for pair in range(R * H // 2):
+                if do_m:
+                    multiply_head(r_m, 2 * pair)
+                if do_t:
+                    transpose_head(r_t, 2 * pair)
+                    transpose_head(r_t, 2 * pair + 1)
+                if do_m:
+                    multiply_head(r_m, 2 * pair + 1)
+
+        def copy_transposed(r):
+            qT_sb[r] = work.tile([P, R, H, P], BF16, name="qT_sb", tag="qT_sb")
+            for i in range(R):
+                nc.scalar.copy(out=qT_sb[r][:, i], in_=qT_ps[r][i][:])
+
+        def scale_and_quantise(r):
+            grouped = work.tile([P, R, PASSES, P, PACK], BF16, name="grouped", tag="grouped", align_bytes=64)
+            for i in range(R):
+                b = place(r, i)[0] // CHUNKS_PER_SEQ
+                for g in range(PASSES):
+                    first = b * H + g * PACK
+                    nc.vector.tensor_tensor(
+                        out=grouped[:, i, g],
+                        in0=ctx_ps[r][i][g][:].rearrange("p t s -> p s t"),
+                        in1=rden[:, first : first + PACK].unsqueeze(1).to_broadcast([P, P, PACK]),
+                        op=mybir.AluOpType.mult,
+                    )
+            codes[r] = work.tile([P, R, PASSES, P], U32, name="codes", tag="codes", align_bytes=64)
+            scales[r] = work.tile([P, R, PASSES, P], U8, name="scales", tag="scales", align_bytes=64)
+            nc.vector.quantize_mx(
+                out=codes[r][:].rearrange("p i g s -> p (i g s)").bitcast(FP8X4),
+                scales=scales[r][:].rearrange("p i g s -> p (i g s)"),
+                in_=grouped[:].rearrange("p i g s t -> p (i g s t)"),
+            )
+
+        def project(r):
+            out_ps[r] = [out_banks.tile([P, E], F32, name="out_ps", tag="out_ps") for i in range(R)]
+            for i in range(R):
+                for g in range(PASSES):
+                    nc.tensor.matmul_mx(
+                        out=out_ps[r][i][:],
+                        lhsT=codes[r][:, i, g, :].bitcast(FP8X4),
+                        lhsT_scale=scales[r][:, i, g, :],
+                        rhs=wo_codes[:, g, :].bitcast(FP8X4),
+                        rhs_scale=wo_scales[:, g, :],
+                        start=(g == 0),
+                        stop=(g == PASSES - 1),
+                    )
+
+        def add_bias_and_store(r):
+            for i in range(R):
+                c, j = place(r, i)
+                slot = j % STORE_J
+                if slot == 0:
+                    out_sb[c] = out_pool.tile([P, STORE_J, E], F32, name="out_sb", tag="out_sb")
+                nc.scalar.copy(out=out_sb[c][:, slot, :], in_=out_ps[r][i][:])
+                nc.gpsimd.tensor_tensor(
+                    out=out_sb[c][:, slot, :], in0=out_sb[c][:, slot, :], in1=bias_sb[:], op=mybir.AluOpType.add
+                )
+                if slot == STORE_J - 1:
+                    b, part = divmod(c, CHUNKS_PER_SEQ)
+                    rows = out[b, part * CHUNK : (part + 1) * CHUNK, :].rearrange("(p j) n -> p j n", j=J)
+                    nc.sync.dma_start(out=rows[:, j - slot : j + 1, :], in_=out_sb[c][:])
+                if j == J - 1 and c + LOADS_AHEAD < N_CHUNKS:
+                    q_tiles[c + LOADS_AHEAD] = load_chunk(c + LOADS_AHEAD)
+
+        for k in range(N_ROUNDS + 2):
+            transposes_and_first_matmul(k, k - 1)
+            if k < N_ROUNDS:
+                copy_transposed(k)
+            if 0 <= k - 1 < N_ROUNDS:
+                scale_and_quantise(k - 1)
+            if k - 2 >= 0:
+                project(k - 2)
+                add_bias_and_store(k - 2)

@@ -13,13 +13,13 @@ P = 128
 B, H, S, DH, E = 2, 8, 4096, 128, 512
 PACK = 4
 PASSES = H // PACK
-J = 8
-CHUNK = P * J
-CHUNKS_PER_SEQ = S // CHUNK
-N_CHUNKS = B * CHUNKS_PER_SEQ
-R = 2
-N_ROUNDS = N_CHUNKS * J // R
-STORE_J = 2
+J = 4
+BLOCK = P * J
+BLOCKS_PER_SEQ = S // BLOCK
+N_BLOCKS = B * BLOCKS_PER_SEQ
+N_UNITS = N_BLOCKS * PASSES
+PAIR = 2
+N_PAIRS = N_BLOCKS * J // PAIR
 LOADS_AHEAD = 4
 
 FLOPS = 2 * B * H * S * DH * DH + 2 * B * S * H * DH * E
@@ -29,18 +29,19 @@ def tile_linearattention_pb_t_kernel(tc, q_feat, kv, denom, Wo, bo, out):
     nc = tc.nc
     with ExitStack() as stack:
         const = stack.enter_context(tc.tile_pool(name="const", bufs=1))
-        q_pool = stack.enter_context(tc.tile_pool(name="q", bufs=N_CHUNKS))
+        q_pool = stack.enter_context(tc.tile_pool(name="q", bufs=LOADS_AHEAD + 2))
         work = stack.enter_context(tc.tile_pool(name="work", bufs=2))
-        out_pool = stack.enter_context(tc.tile_pool(name="outs", bufs=6))
-        qT_banks = stack.enter_context(tc.psum_pool(name="qT_banks", bufs=R))
-        ctx_banks = stack.enter_context(tc.psum_pool(name="ctx_banks", bufs=R * PASSES))
-        out_banks = stack.enter_context(tc.psum_pool(name="out_banks", bufs=R))
+        mx_pool = stack.enter_context(tc.tile_pool(name="mx", bufs=4))
+        out_pool = stack.enter_context(tc.tile_pool(name="outs", bufs=4))
+        qT_banks = stack.enter_context(tc.psum_pool(name="qT_banks", bufs=2))
+        ctx_banks = stack.enter_context(tc.psum_pool(name="ctx_banks", bufs=PACK))
+        out_banks = stack.enter_context(tc.psum_pool(name="out_banks", bufs=PAIR))
         stack.enter_context(tc.manual_schedule())
 
-        def load_chunk(c):
-            b, part = divmod(c, CHUNKS_PER_SEQ)
+        def load_block(blk):
+            b, part = divmod(blk, BLOCKS_PER_SEQ)
             q_sb = q_pool.tile([P, H, J * DH], BF16, name="q_sb", tag="q_sb")
-            rows = q_feat[b, :, part * CHUNK : (part + 1) * CHUNK, :]
+            rows = q_feat[b, :, part * BLOCK : (part + 1) * BLOCK, :]
             nc.sync.dma_start(out=q_sb[:], in_=rows.rearrange("h (p j) d -> p h (j d)", j=J))
             return q_sb
 
@@ -48,145 +49,159 @@ def tile_linearattention_pb_t_kernel(tc, q_feat, kv, denom, Wo, bo, out):
         nc.vector.memset(bias_row[:], 0.0)
         denom_bc = const.tile([P, B * H], BF16)
         nc.sync.dma_start(out=denom_bc[:], in_=denom.rearrange("b h x y -> (b h x y)").partition_broadcast(P))
-        wo_raw = const.tile([P, H, E], BF16)
-        nc.sync.dma_start(out=wo_raw[:], in_=Wo.rearrange("(c p) n -> p c n", p=P))
         kv_sb = const.tile([P, B, H, DH], BF16)
         nc.sync.dma_start(out=kv_sb[:, 0], in_=kv[0].rearrange("h d e -> d h e"))
+        q_tiles = {0: load_block(0)}
         nc.sync.dma_start(out=bias_row[0:1, :], in_=bo.rearrange("(o n) -> o n", o=1))
-        q_tiles = {}
-        for c in range(LOADS_AHEAD):
-            q_tiles[c] = load_chunk(c)
+        wo_raw = const.tile([P, H, E], BF16)
+        nc.sync.dma_start(out=wo_raw[:], in_=Wo.rearrange("(c p) n -> p c n", p=P))
+        for blk in range(1, LOADS_AHEAD):
+            q_tiles[blk] = load_block(blk)
         nc.sync.dma_start(out=kv_sb[:, 1], in_=kv[1].rearrange("h d e -> d h e"))
 
         identity = const.tile([P, P], BF16)
         masks.make_identity(nc, identity[:])
         ones = const.tile([P, P], BF16)
-        nc.vector.memset(ones[:], 1.0)
         rden = const.tile([P, B * H], F32)
-        nc.vector.reciprocal(out=rden[:], in_=denom_bc[:])
-
+        bias_sb = const.tile([P, E], F32)
         wo_grouped = const.tile([P, PASSES, E, PACK], BF16, align_bytes=64)
-        for g in range(PASSES):
-            nc.vector.tensor_copy(
-                out=wo_grouped[:, g],
-                in_=wo_raw[:, g * PACK : (g + 1) * PACK, :].rearrange("p t n -> p n t"),
-            )
         wo_codes = const.tile([P, PASSES, E], U32, align_bytes=64)
         wo_scales = const.tile([P, PASSES, E], U8, align_bytes=64)
-        nc.vector.quantize_mx(
-            out=wo_codes[:].rearrange("p g n -> p (g n)").bitcast(FP8X4),
-            scales=wo_scales[:].rearrange("p g n -> p (g n)"),
-            in_=wo_grouped[:].rearrange("p g n t -> p (g n t)"),
-        )
 
-        bias_ps = out_banks.tile([P, E], F32, name="bias_ps", tag="out_ps")
-        nc.tensor.matmul(out=bias_ps[:], lhsT=ones[:], rhs=bias_row[:], start=True, stop=True)
-        bias_sb = const.tile([P, E], F32)
-        nc.vector.tensor_copy(out=bias_sb[:], in_=bias_ps[:])
-
-        qT_ps, qT_sb, ctx_ps, codes, scales, out_ps, out_sb = {}, {}, {}, {}, {}, {}, {}
-
-        def place(r, i):
-            return divmod(r * R + i, J)
-
-        def transpose_head(r, u):
-            i, h = divmod(u, H)
-            c, j = place(r, i)
-            nc.tensor.transpose(qT_ps[r][i][:, h, :], q_tiles[c][:, h, j * DH : (j + 1) * DH], identity[:])
-
-        def multiply_head(r, u):
-            i, h = divmod(u, H)
-            g, t = divmod(h, PACK)
-            b = place(r, i)[0] // CHUNKS_PER_SEQ
-            nc.tensor.matmul(
-                out=ctx_ps[r][i][g][:, t, :],
-                lhsT=kv_sb[:, b, h, :],
-                rhs=qT_sb[r][:, i, h, :],
-                start=True,
-                stop=True,
-            )
-
-        def transposes_and_first_matmul(r_t, r_m):
-            do_t = r_t < N_ROUNDS
-            do_m = 0 <= r_m < N_ROUNDS
-            if do_t:
-                qT_ps[r_t] = [qT_banks.tile([P, H, P], BF16, name="qT_ps", tag="qT_ps") for i in range(R)]
-            if do_m:
-                ctx_ps[r_m] = [
-                    [ctx_banks.tile([P, PACK, P], F32, name="ctx_ps", tag="ctx_ps") for g in range(PASSES)]
-                    for i in range(R)
-                ]
-            for pair in range(R * H // 2):
-                if do_m:
-                    multiply_head(r_m, 2 * pair)
-                if do_t:
-                    transpose_head(r_t, 2 * pair)
-                    transpose_head(r_t, 2 * pair + 1)
-                if do_m:
-                    multiply_head(r_m, 2 * pair + 1)
-
-        def copy_transposed(r):
-            qT_sb[r] = work.tile([P, R, H, P], BF16, name="qT_sb", tag="qT_sb")
-            for i in range(R):
-                nc.scalar.copy(out=qT_sb[r][:, i], in_=qT_ps[r][i][:])
-
-        def scale_and_quantise(r):
-            grouped = work.tile([P, R, PASSES, P, PACK], BF16, name="grouped", tag="grouped", align_bytes=64)
-            for i in range(R):
-                b = place(r, i)[0] // CHUNKS_PER_SEQ
-                for g in range(PASSES):
-                    first = b * H + g * PACK
-                    nc.vector.tensor_tensor(
-                        out=grouped[:, i, g],
-                        in0=ctx_ps[r][i][g][:].rearrange("p t s -> p s t"),
-                        in1=rden[:, first : first + PACK].unsqueeze(1).to_broadcast([P, P, PACK]),
-                        op=mybir.AluOpType.mult,
-                    )
-            codes[r] = work.tile([P, R, PASSES, P], U32, name="codes", tag="codes", align_bytes=64)
-            scales[r] = work.tile([P, R, PASSES, P], U8, name="scales", tag="scales", align_bytes=64)
+        def prepare_constants():
+            nc.vector.reciprocal(out=rden[:], in_=denom_bc[:])
+            nc.vector.memset(ones[:], 1.0)
+            bias_ps = out_banks.tile([P, E], F32, name="bias_ps", tag="out_ps")
+            nc.tensor.matmul(out=bias_ps[:], lhsT=ones[:], rhs=bias_row[:], start=True, stop=True)
+            nc.vector.tensor_copy(out=bias_sb[:], in_=bias_ps[:])
+            for g in range(PASSES):
+                nc.vector.tensor_copy(
+                    out=wo_grouped[:, g],
+                    in_=wo_raw[:, g * PACK : (g + 1) * PACK, :].rearrange("p t n -> p n t"),
+                )
             nc.vector.quantize_mx(
-                out=codes[r][:].rearrange("p i g s -> p (i g s)").bitcast(FP8X4),
-                scales=scales[r][:].rearrange("p i g s -> p (i g s)"),
-                in_=grouped[:].rearrange("p i g s t -> p (i g s t)"),
+                out=wo_codes[:].rearrange("p g n -> p (g n)").bitcast(FP8X4),
+                scales=wo_scales[:].rearrange("p g n -> p (g n)"),
+                in_=wo_grouped[:].rearrange("p g n t -> p (g n t)"),
             )
 
-        def project(r):
-            out_ps[r] = [out_banks.tile([P, E], F32, name="out_ps", tag="out_ps") for i in range(R)]
-            for i in range(R):
+        qT_ps, qT_sb, ctx_ps, ctx_sb, grouped, codes, scales, out_ps, out_sb = {}, {}, {}, {}, {}, {}, {}, {}, {}
+
+        def is_unit(u):
+            return 0 <= u < N_UNITS
+
+        def transposes_and_plain_matmuls(u_t, u_m):
+            if is_unit(u_t):
+                qT_ps[u_t] = [qT_banks.tile([P, 2, BLOCK], BF16, name="qT_ps", tag="qT_ps") for half in range(2)]
+            for t in range(PACK):
+                if is_unit(u_m):
+                    blk, g = divmod(u_m, PASSES)
+                    ctx_ps[u_m, t] = ctx_banks.tile([P, BLOCK], F32, name="ctx_ps", tag="ctx_ps")
+                    nc.tensor.matmul(
+                        out=ctx_ps[u_m, t][:],
+                        lhsT=kv_sb[:, blk // BLOCKS_PER_SEQ, g * PACK + t, :],
+                        rhs=qT_sb[u_m][:, t, :],
+                        start=True,
+                        stop=True,
+                    )
+                if is_unit(u_t):
+                    blk, g = divmod(u_t, PASSES)
+                    for j in range(J):
+                        nc.tensor.transpose(
+                            qT_ps[u_t][t // 2][:, t % 2, j * P : (j + 1) * P],
+                            q_tiles[blk][:, g * PACK + t, j * DH : (j + 1) * DH],
+                            identity[:],
+                        )
+
+        def divide_head(u, t):
+            blk, g = divmod(u, PASSES)
+            head = (blk // BLOCKS_PER_SEQ) * H + g * PACK + t
+            if u % 2 == 1 and t == PACK - 1:
+                nc.vector.tensor_scalar_mul(out=ctx_sb[u][:, t, :], in0=ctx_ps[u, t][:], scalar1=rden[:, head : head + 1])
+            else:
+                nc.scalar.activation(
+                    out=ctx_sb[u][:, t, :],
+                    in_=ctx_ps[u, t][:],
+                    func=mybir.ActivationFunctionType.Copy,
+                    scale=rden[:, head : head + 1],
+                )
+
+        def leave_psum(u_t, u_m):
+            if is_unit(u_t):
+                qT_sb[u_t] = work.tile([P, PACK, BLOCK], BF16, name="qT_sb", tag="qT_sb")
+            if is_unit(u_m):
+                ctx_sb[u_m] = work.tile([P, PACK, BLOCK], BF16, name="ctx_sb", tag="ctx_sb")
+            for half in range(2):
+                if is_unit(u_m):
+                    divide_head(u_m, 2 * half)
+                    divide_head(u_m, 2 * half + 1)
+                if is_unit(u_t):
+                    nc.scalar.copy(out=qT_sb[u_t][:, 2 * half : 2 * half + 2, :], in_=qT_ps[u_t][half][:])
+
+        def regroup(u):
+            if not is_unit(u):
+                return
+            grouped[u] = work.tile([P, BLOCK, PACK], BF16, name="grouped", tag="grouped", align_bytes=64)
+            nc.vector.tensor_copy(
+                out=grouped[u][:].rearrange("p (c i) t -> p c t i", i=4),
+                in_=ctx_sb[u][:].rearrange("p t (c i) -> p c t i", i=4),
+            )
+
+        def quantise(u):
+            if not is_unit(u):
+                return
+            codes[u] = mx_pool.tile([P, BLOCK], U32, name="codes", tag="codes", align_bytes=64)
+            scales[u] = mx_pool.tile([P, BLOCK], U8, name="scales", tag="scales", align_bytes=64)
+            nc.vector.quantize_mx(
+                out=codes[u][:].bitcast(FP8X4),
+                scales=scales[u][:],
+                in_=grouped[u][:].rearrange("p s t -> p (s t)"),
+            )
+
+        def project(pair):
+            blk, second = divmod(pair, J // PAIR)
+            out_ps[pair] = [out_banks.tile([P, E], F32, name="out_ps", tag="out_ps") for i in range(PAIR)]
+            for i in range(PAIR):
+                cols = slice((second * PAIR + i) * P, (second * PAIR + i + 1) * P)
                 for g in range(PASSES):
                     nc.tensor.matmul_mx(
-                        out=out_ps[r][i][:],
-                        lhsT=codes[r][:, i, g, :].bitcast(FP8X4),
-                        lhsT_scale=scales[r][:, i, g, :],
+                        out=out_ps[pair][i][:],
+                        lhsT=codes[blk * PASSES + g][:, cols].bitcast(FP8X4),
+                        lhsT_scale=scales[blk * PASSES + g][:, cols],
                         rhs=wo_codes[:, g, :].bitcast(FP8X4),
                         rhs_scale=wo_scales[:, g, :],
                         start=(g == 0),
                         stop=(g == PASSES - 1),
                     )
 
-        def add_bias_and_store(r):
-            for i in range(R):
-                c, j = place(r, i)
-                slot = j % STORE_J
-                if slot == 0:
-                    out_sb[c] = out_pool.tile([P, STORE_J, E], F32, name="out_sb", tag="out_sb")
-                nc.scalar.copy(out=out_sb[c][:, slot, :], in_=out_ps[r][i][:])
-                nc.gpsimd.tensor_tensor(
-                    out=out_sb[c][:, slot, :], in0=out_sb[c][:, slot, :], in1=bias_sb[:], op=mybir.AluOpType.add
-                )
-                if slot == STORE_J - 1:
-                    b, part = divmod(c, CHUNKS_PER_SEQ)
-                    rows = out[b, part * CHUNK : (part + 1) * CHUNK, :].rearrange("(p j) n -> p j n", j=J)
-                    nc.sync.dma_start(out=rows[:, j - slot : j + 1, :], in_=out_sb[c][:])
-                if j == J - 1 and c + LOADS_AHEAD < N_CHUNKS:
-                    q_tiles[c + LOADS_AHEAD] = load_chunk(c + LOADS_AHEAD)
+        def add_bias(pair, i):
+            nc.vector.tensor_tensor(
+                out=out_sb[pair][:, i, :], in0=out_ps[pair][i][:], in1=bias_sb[:], op=mybir.AluOpType.add
+            )
 
-        for k in range(N_ROUNDS + 2):
-            transposes_and_first_matmul(k, k - 1)
-            if k < N_ROUNDS:
-                copy_transposed(k)
-            if 0 <= k - 1 < N_ROUNDS:
-                scale_and_quantise(k - 1)
-            if k - 2 >= 0:
-                project(k - 2)
-                add_bias_and_store(k - 2)
+        def store(pair):
+            blk, second = divmod(pair, J // PAIR)
+            b, part = divmod(blk, BLOCKS_PER_SEQ)
+            rows = out[b, part * BLOCK : (part + 1) * BLOCK, :].rearrange("(p j) n -> p j n", j=J)
+            nc.sync.dma_start(out=rows[:, second * PAIR : (second + 1) * PAIR, :], in_=out_sb[pair][:])
+            if second == J // PAIR - 1 and blk + LOADS_AHEAD < N_BLOCKS:
+                q_tiles[blk + LOADS_AHEAD] = load_block(blk + LOADS_AHEAD)
+
+        def pipeline_step(step):
+            transposes_and_plain_matmuls(step, step - 1)
+            pair = step - 4
+            if 0 <= pair < N_PAIRS:
+                project(pair)
+                out_sb[pair] = out_pool.tile([P, PAIR, E], F32, name="out_sb", tag="out_sb")
+                add_bias(pair, 0)
+            quantise(step - 2)
+            if 0 <= pair < N_PAIRS:
+                add_bias(pair, 1)
+                store(pair)
+            leave_psum(step, step - 1)
+            regroup(step - 1)
+
+        pipeline_step(0)
+        prepare_constants()
+        for step in range(1, N_PAIRS + 4):
+            pipeline_step(step)

@@ -18,9 +18,11 @@ BLOCK = P * J
 BLOCKS_PER_SEQ = S // BLOCK
 N_BLOCKS = B * BLOCKS_PER_SEQ
 N_UNITS = N_BLOCKS * PASSES
+HEADS_PER_BANK = 2
 PAIR = 2
 N_PAIRS = N_BLOCKS * J // PAIR
-LOADS_AHEAD = 4
+LOADS_AHEAD = 8
+PROJECT_LAG = 4
 
 FLOPS = 2 * B * H * S * DH * DH + 2 * B * S * H * DH * E
 
@@ -29,56 +31,62 @@ def tile_linearattention_pb_t_kernel(tc, q_feat, kv, denom, Wo, bo, out):
     nc = tc.nc
     with ExitStack() as stack:
         const = stack.enter_context(tc.tile_pool(name="const", bufs=1))
-        q_pool = stack.enter_context(tc.tile_pool(name="q", bufs=LOADS_AHEAD + 2))
+        q_pool = stack.enter_context(tc.tile_pool(name="q", bufs=LOADS_AHEAD + PROJECT_LAG))
         work = stack.enter_context(tc.tile_pool(name="work", bufs=2))
         mx_pool = stack.enter_context(tc.tile_pool(name="mx", bufs=4))
         out_pool = stack.enter_context(tc.tile_pool(name="outs", bufs=4))
-        qT_banks = stack.enter_context(tc.psum_pool(name="qT_banks", bufs=2))
+        qT_banks = stack.enter_context(tc.psum_pool(name="qT_banks", bufs=PACK // HEADS_PER_BANK))
         ctx_banks = stack.enter_context(tc.psum_pool(name="ctx_banks", bufs=PACK))
         out_banks = stack.enter_context(tc.psum_pool(name="out_banks", bufs=PAIR))
         stack.enter_context(tc.manual_schedule())
 
-        def load_block(blk):
+        q_tiles = {}
+
+        def load_unit(u):
+            blk, g = divmod(u, PASSES)
             b, part = divmod(blk, BLOCKS_PER_SEQ)
-            q_sb = q_pool.tile([P, H, J * DH], BF16, name="q_sb", tag="q_sb")
-            rows = q_feat[b, :, part * BLOCK : (part + 1) * BLOCK, :]
-            nc.sync.dma_start(out=q_sb[:], in_=rows.rearrange("h (p j) d -> p h (j d)", j=J))
-            return q_sb
+            q_tiles[u] = q_pool.tile([P, PACK, J * DH], BF16, name="q_sb", tag="q_sb")
+            rows = q_feat[b, g * PACK : (g + 1) * PACK, part * BLOCK : (part + 1) * BLOCK, :]
+            nc.sync.dma_start(out=q_tiles[u][:], in_=rows.rearrange("h (p j) d -> p h (j d)", j=J))
 
         bias_row = const.tile([P, E], BF16)
         nc.vector.memset(bias_row[:], 0.0)
-        denom_bc = const.tile([P, B * H], BF16)
-        nc.sync.dma_start(out=denom_bc[:], in_=denom.rearrange("b h x y -> (b h x y)").partition_broadcast(P))
+        ones = const.tile([P, P], BF16)
+        nc.vector.memset(ones[:], 1.0)
+        identity = const.tile([P, P], BF16)
+        masks.make_identity(nc, identity[:])
+
+        load_unit(0)
         kv_sb = const.tile([P, B, H, DH], BF16)
         nc.sync.dma_start(out=kv_sb[:, 0], in_=kv[0].rearrange("h d e -> d h e"))
-        q_tiles = {0: load_block(0)}
+        denom_bc = const.tile([P, B * H], BF16)
+        nc.sync.dma_start(out=denom_bc[:], in_=denom.rearrange("b h x y -> (b h x y)").partition_broadcast(P))
+        load_unit(1)
+        load_unit(2)
         nc.sync.dma_start(out=bias_row[0:1, :], in_=bo.rearrange("(o n) -> o n", o=1))
         wo_raw = const.tile([P, H, E], BF16)
         nc.sync.dma_start(out=wo_raw[:], in_=Wo.rearrange("(c p) n -> p c n", p=P))
-        for blk in range(1, LOADS_AHEAD):
-            q_tiles[blk] = load_block(blk)
+        for u in range(3, LOADS_AHEAD):
+            load_unit(u)
         nc.sync.dma_start(out=kv_sb[:, 1], in_=kv[1].rearrange("h d e -> d h e"))
 
-        identity = const.tile([P, P], BF16)
-        masks.make_identity(nc, identity[:])
-        ones = const.tile([P, P], BF16)
         rden = const.tile([P, B * H], F32)
         bias_sb = const.tile([P, E], F32)
         wo_grouped = const.tile([P, PASSES, E, PACK], BF16, align_bytes=64)
         wo_codes = const.tile([P, PASSES, E], U32, align_bytes=64)
         wo_scales = const.tile([P, PASSES, E], U8, align_bytes=64)
 
-        def prepare_constants():
-            nc.vector.reciprocal(out=rden[:], in_=denom_bc[:])
-            nc.vector.memset(ones[:], 1.0)
+        def side_by_side(dst, src):
+            nc.vector.tensor_copy(
+                out=dst.rearrange("p (c i) t -> p c t i", i=4), in_=src.rearrange("p t (c i) -> p c t i", i=4)
+            )
+
+        def prepare_projection():
             bias_ps = out_banks.tile([P, E], F32, name="bias_ps", tag="out_ps")
             nc.tensor.matmul(out=bias_ps[:], lhsT=ones[:], rhs=bias_row[:], start=True, stop=True)
             nc.vector.tensor_copy(out=bias_sb[:], in_=bias_ps[:])
             for g in range(PASSES):
-                nc.vector.tensor_copy(
-                    out=wo_grouped[:, g],
-                    in_=wo_raw[:, g * PACK : (g + 1) * PACK, :].rearrange("p t n -> p n t"),
-                )
+                side_by_side(wo_grouped[:, g], wo_raw[:, g * PACK : (g + 1) * PACK, :])
             nc.vector.quantize_mx(
                 out=wo_codes[:].rearrange("p g n -> p (g n)").bitcast(FP8X4),
                 scales=wo_scales[:].rearrange("p g n -> p (g n)"),
@@ -90,33 +98,47 @@ def tile_linearattention_pb_t_kernel(tc, q_feat, kv, denom, Wo, bo, out):
         def is_unit(u):
             return 0 <= u < N_UNITS
 
-        def transposes_and_plain_matmuls(u_t, u_m):
-            if is_unit(u_t):
-                qT_ps[u_t] = [qT_banks.tile([P, 2, BLOCK], BF16, name="qT_ps", tag="qT_ps") for half in range(2)]
+        def plain_matmul(u, t):
+            blk, g = divmod(u, PASSES)
+            ctx_ps[u, t] = ctx_banks.tile([P, BLOCK], F32, name="ctx_ps", tag="ctx_ps")
+            nc.tensor.matmul(
+                out=ctx_ps[u, t][:],
+                lhsT=kv_sb[:, blk // BLOCKS_PER_SEQ, g * PACK + t, :],
+                rhs=qT_sb[u][:, t, :],
+                start=True,
+                stop=True,
+            )
+
+        def transpose_unit(u):
+            qT_ps[u] = [
+                qT_banks.tile([P, HEADS_PER_BANK, BLOCK], BF16, name="qT_ps", tag="qT_ps")
+                for bank in range(PACK // HEADS_PER_BANK)
+            ]
             for t in range(PACK):
-                if is_unit(u_m):
-                    blk, g = divmod(u_m, PASSES)
-                    ctx_ps[u_m, t] = ctx_banks.tile([P, BLOCK], F32, name="ctx_ps", tag="ctx_ps")
-                    nc.tensor.matmul(
-                        out=ctx_ps[u_m, t][:],
-                        lhsT=kv_sb[:, blk // BLOCKS_PER_SEQ, g * PACK + t, :],
-                        rhs=qT_sb[u_m][:, t, :],
-                        start=True,
-                        stop=True,
+                for j in range(J):
+                    nc.tensor.transpose(
+                        qT_ps[u][t // HEADS_PER_BANK][:, t % HEADS_PER_BANK, j * P : (j + 1) * P],
+                        q_tiles[u][:, t, j * DH : (j + 1) * DH],
+                        identity[:],
                     )
-                if is_unit(u_t):
-                    blk, g = divmod(u_t, PASSES)
-                    for j in range(J):
-                        nc.tensor.transpose(
-                            qT_ps[u_t][t // 2][:, t % 2, j * P : (j + 1) * P],
-                            q_tiles[blk][:, g * PACK + t, j * DH : (j + 1) * DH],
-                            identity[:],
-                        )
+
+        def transposes_and_plain_matmuls(u_t, u_m):
+            if is_unit(u_m):
+                plain_matmul(u_m, 0)
+                plain_matmul(u_m, 1)
+            if is_unit(u_t):
+                transpose_unit(u_t)
+            if is_unit(u_m):
+                plain_matmul(u_m, 2)
+                plain_matmul(u_m, 3)
+
+        def heads_on_vector(u):
+            return 2 if u == 0 else u % 2
 
         def divide_head(u, t):
             blk, g = divmod(u, PASSES)
             head = (blk // BLOCKS_PER_SEQ) * H + g * PACK + t
-            if u % 2 == 1 and t == PACK - 1:
+            if t >= PACK - heads_on_vector(u):
                 nc.vector.tensor_scalar_mul(out=ctx_sb[u][:, t, :], in0=ctx_ps[u, t][:], scalar1=rden[:, head : head + 1])
             else:
                 nc.scalar.activation(
@@ -127,36 +149,33 @@ def tile_linearattention_pb_t_kernel(tc, q_feat, kv, denom, Wo, bo, out):
                 )
 
         def leave_psum(u_t, u_m):
-            if is_unit(u_t):
-                qT_sb[u_t] = work.tile([P, PACK, BLOCK], BF16, name="qT_sb", tag="qT_sb")
             if is_unit(u_m):
                 ctx_sb[u_m] = work.tile([P, PACK, BLOCK], BF16, name="ctx_sb", tag="ctx_sb")
-            for half in range(2):
-                if is_unit(u_m):
-                    divide_head(u_m, 2 * half)
-                    divide_head(u_m, 2 * half + 1)
-                if is_unit(u_t):
-                    nc.scalar.copy(out=qT_sb[u_t][:, 2 * half : 2 * half + 2, :], in_=qT_ps[u_t][half][:])
+                divide_head(u_m, 0)
+                divide_head(u_m, 1)
+            if is_unit(u_t):
+                qT_sb[u_t] = work.tile([P, PACK, BLOCK], BF16, name="qT_sb", tag="qT_sb")
+                for bank in range(PACK // HEADS_PER_BANK):
+                    heads = slice(bank * HEADS_PER_BANK, (bank + 1) * HEADS_PER_BANK)
+                    nc.scalar.copy(out=qT_sb[u_t][:, heads, :], in_=qT_ps[u_t][bank][:])
+            if is_unit(u_m):
+                divide_head(u_m, 2)
+                divide_head(u_m, 3)
 
         def regroup(u):
-            if not is_unit(u):
-                return
-            grouped[u] = work.tile([P, BLOCK, PACK], BF16, name="grouped", tag="grouped", align_bytes=64)
-            nc.vector.tensor_copy(
-                out=grouped[u][:].rearrange("p (c i) t -> p c t i", i=4),
-                in_=ctx_sb[u][:].rearrange("p t (c i) -> p c t i", i=4),
-            )
+            if is_unit(u):
+                grouped[u] = work.tile([P, BLOCK, PACK], BF16, name="grouped", tag="grouped", align_bytes=64)
+                side_by_side(grouped[u][:], ctx_sb[u][:])
 
         def quantise(u):
-            if not is_unit(u):
-                return
-            codes[u] = mx_pool.tile([P, BLOCK], U32, name="codes", tag="codes", align_bytes=64)
-            scales[u] = mx_pool.tile([P, BLOCK], U8, name="scales", tag="scales", align_bytes=64)
-            nc.vector.quantize_mx(
-                out=codes[u][:].bitcast(FP8X4),
-                scales=scales[u][:],
-                in_=grouped[u][:].rearrange("p s t -> p (s t)"),
-            )
+            if is_unit(u):
+                codes[u] = mx_pool.tile([P, BLOCK], U32, name="codes", tag="codes", align_bytes=64)
+                scales[u] = mx_pool.tile([P, BLOCK], U8, name="scales", tag="scales", align_bytes=64)
+                nc.vector.quantize_mx(
+                    out=codes[u][:].bitcast(FP8X4),
+                    scales=scales[u][:],
+                    in_=grouped[u][:].rearrange("p s t -> p (s t)"),
+                )
 
         def project(pair):
             blk, second = divmod(pair, J // PAIR)
@@ -174,34 +193,33 @@ def tile_linearattention_pb_t_kernel(tc, q_feat, kv, denom, Wo, bo, out):
                         stop=(g == PASSES - 1),
                     )
 
-        def add_bias(pair, i):
+        def add_bias_and_store(pair, i):
             nc.vector.tensor_tensor(
                 out=out_sb[pair][:, i, :], in0=out_ps[pair][i][:], in1=bias_sb[:], op=mybir.AluOpType.add
             )
-
-        def store(pair):
             blk, second = divmod(pair, J // PAIR)
             b, part = divmod(blk, BLOCKS_PER_SEQ)
             rows = out[b, part * BLOCK : (part + 1) * BLOCK, :].rearrange("(p j) n -> p j n", j=J)
-            nc.sync.dma_start(out=rows[:, second * PAIR : (second + 1) * PAIR, :], in_=out_sb[pair][:])
-            if second == J // PAIR - 1 and blk + LOADS_AHEAD < N_BLOCKS:
-                q_tiles[blk + LOADS_AHEAD] = load_block(blk + LOADS_AHEAD)
+            nc.sync.dma_start(out=rows[:, second * PAIR + i, :], in_=out_sb[pair][:, i, :])
 
         def pipeline_step(step):
             transposes_and_plain_matmuls(step, step - 1)
-            pair = step - 4
+            pair = step - PROJECT_LAG
             if 0 <= pair < N_PAIRS:
                 project(pair)
                 out_sb[pair] = out_pool.tile([P, PAIR, E], F32, name="out_sb", tag="out_sb")
-                add_bias(pair, 0)
+                add_bias_and_store(pair, 0)
             quantise(step - 2)
             if 0 <= pair < N_PAIRS:
-                add_bias(pair, 1)
-                store(pair)
+                add_bias_and_store(pair, 1)
+                if is_unit(pair + LOADS_AHEAD):
+                    load_unit(pair + LOADS_AHEAD)
             leave_psum(step, step - 1)
             regroup(step - 1)
 
-        pipeline_step(0)
-        prepare_constants()
-        for step in range(1, N_PAIRS + 4):
+        for step in range(N_PAIRS + PROJECT_LAG):
             pipeline_step(step)
+            if step == 0:
+                nc.vector.reciprocal(out=rden[:], in_=denom_bc[:])
+            if step == PROJECT_LAG - 2:
+                prepare_projection()

@@ -16,13 +16,11 @@ PASSES = H // PACK
 J = 4
 BLOCK = P * J
 BLOCKS_PER_SEQ = S // BLOCK
-N_BLOCKS = B * BLOCKS_PER_SEQ
-N_UNITS = N_BLOCKS * PASSES
-HEADS_PER_BANK = 2
-PAIR = 2
-N_PAIRS = N_BLOCKS * J // PAIR
+N_LOADS = B * BLOCKS_PER_SEQ * PASSES
+R = 2
+ROUNDS_PER_BLOCK = J // R
+N_ROUNDS = B * S // (R * P)
 LOADS_AHEAD = 8
-PROJECT_LAG = 4
 
 FLOPS = 2 * B * H * S * DH * DH + 2 * B * S * H * DH * E
 
@@ -31,23 +29,23 @@ def tile_linearattention_pb_t_kernel(tc, q_feat, kv, denom, Wo, bo, out):
     nc = tc.nc
     with ExitStack() as stack:
         const = stack.enter_context(tc.tile_pool(name="const", bufs=1))
-        q_pool = stack.enter_context(tc.tile_pool(name="q", bufs=LOADS_AHEAD + PROJECT_LAG))
+        q_pool = stack.enter_context(tc.tile_pool(name="q", bufs=LOADS_AHEAD + 4))
         work = stack.enter_context(tc.tile_pool(name="work", bufs=2))
-        mx_pool = stack.enter_context(tc.tile_pool(name="mx", bufs=4))
+        mx_pool = stack.enter_context(tc.tile_pool(name="mx", bufs=3))
         out_pool = stack.enter_context(tc.tile_pool(name="outs", bufs=4))
-        qT_banks = stack.enter_context(tc.psum_pool(name="qT_banks", bufs=PACK // HEADS_PER_BANK))
-        ctx_banks = stack.enter_context(tc.psum_pool(name="ctx_banks", bufs=PACK))
-        out_banks = stack.enter_context(tc.psum_pool(name="out_banks", bufs=PAIR))
+        qT_banks = stack.enter_context(tc.psum_pool(name="qT_banks", bufs=R))
+        ctx_banks = stack.enter_context(tc.psum_pool(name="ctx_banks", bufs=R * PASSES))
+        out_banks = stack.enter_context(tc.psum_pool(name="out_banks", bufs=R))
         stack.enter_context(tc.manual_schedule())
 
         q_tiles = {}
 
-        def load_unit(u):
-            blk, g = divmod(u, PASSES)
+        def load_q(n):
+            blk, g = divmod(n, PASSES)
             b, part = divmod(blk, BLOCKS_PER_SEQ)
-            q_tiles[u] = q_pool.tile([P, PACK, J * DH], BF16, name="q_sb", tag="q_sb")
+            q_tiles[n] = q_pool.tile([P, PACK, J * DH], BF16, name="q_sb", tag="q_sb")
             rows = q_feat[b, g * PACK : (g + 1) * PACK, part * BLOCK : (part + 1) * BLOCK, :]
-            nc.sync.dma_start(out=q_tiles[u][:], in_=rows.rearrange("h (p j) d -> p h (j d)", j=J))
+            nc.sync.dma_start(out=q_tiles[n][:], in_=rows.rearrange("h (p j) d -> p h (j d)", j=J))
 
         bias_row = const.tile([P, E], BF16)
         nc.vector.memset(bias_row[:], 0.0)
@@ -56,18 +54,17 @@ def tile_linearattention_pb_t_kernel(tc, q_feat, kv, denom, Wo, bo, out):
         identity = const.tile([P, P], BF16)
         masks.make_identity(nc, identity[:])
 
-        load_unit(0)
+        load_q(0)
+        load_q(1)
         kv_sb = const.tile([P, B, H, DH], BF16)
         nc.sync.dma_start(out=kv_sb[:, 0], in_=kv[0].rearrange("h d e -> d h e"))
         denom_bc = const.tile([P, B * H], BF16)
         nc.sync.dma_start(out=denom_bc[:], in_=denom.rearrange("b h x y -> (b h x y)").partition_broadcast(P))
-        load_unit(1)
-        load_unit(2)
         nc.sync.dma_start(out=bias_row[0:1, :], in_=bo.rearrange("(o n) -> o n", o=1))
         wo_raw = const.tile([P, H, E], BF16)
         nc.sync.dma_start(out=wo_raw[:], in_=Wo.rearrange("(c p) n -> p c n", p=P))
-        for u in range(3, LOADS_AHEAD):
-            load_unit(u)
+        for n in range(2, LOADS_AHEAD):
+            load_q(n)
         nc.sync.dma_start(out=kv_sb[:, 1], in_=kv[1].rearrange("h d e -> d h e"))
 
         rden = const.tile([P, B * H], F32)
@@ -76,150 +73,146 @@ def tile_linearattention_pb_t_kernel(tc, q_feat, kv, denom, Wo, bo, out):
         wo_codes = const.tile([P, PASSES, E], U32, align_bytes=64)
         wo_scales = const.tile([P, PASSES, E], U8, align_bytes=64)
 
-        def side_by_side(dst, src):
-            nc.vector.tensor_copy(
-                out=dst.rearrange("p (c i) t -> p c t i", i=4), in_=src.rearrange("p t (c i) -> p c t i", i=4)
-            )
-
-        def prepare_projection():
+        def spread_bias():
             bias_ps = out_banks.tile([P, E], F32, name="bias_ps", tag="out_ps")
             nc.tensor.matmul(out=bias_ps[:], lhsT=ones[:], rhs=bias_row[:], start=True, stop=True)
-            nc.vector.tensor_copy(out=bias_sb[:], in_=bias_ps[:])
-            for g in range(PASSES):
-                side_by_side(wo_grouped[:, g], wo_raw[:, g * PACK : (g + 1) * PACK, :])
-            nc.vector.quantize_mx(
-                out=wo_codes[:].rearrange("p g n -> p (g n)").bitcast(FP8X4),
-                scales=wo_scales[:].rearrange("p g n -> p (g n)"),
-                in_=wo_grouped[:].rearrange("p g n t -> p (g n t)"),
+            nc.scalar.copy(out=bias_sb[:], in_=bias_ps[:])
+
+        def regroup_wo(g):
+            nc.scalar.copy(
+                out=wo_grouped[:, g].rearrange("p (c i) t -> p c t i", i=4),
+                in_=wo_raw[:, g * PACK : (g + 1) * PACK, :].rearrange("p t (c i) -> p c t i", i=4),
             )
 
-        qT_ps, qT_sb, ctx_ps, ctx_sb, grouped, codes, scales, out_ps, out_sb = {}, {}, {}, {}, {}, {}, {}, {}, {}
+        def quantise_wo(g):
+            nc.vector.quantize_mx(
+                out=wo_codes[:, g, :].bitcast(FP8X4),
+                scales=wo_scales[:, g, :],
+                in_=wo_grouped[:, g].rearrange("p n t -> p (n t)"),
+            )
 
-        def is_unit(u):
-            return 0 <= u < N_UNITS
+        qT_ps, qT_sb, ctx_ps, grouped, codes, scales, out_ps, out_sb = {}, {}, {}, {}, {}, {}, {}, {}
 
-        def plain_matmul(u, t):
-            blk, g = divmod(u, PASSES)
-            ctx_ps[u, t] = ctx_banks.tile([P, BLOCK], F32, name="ctx_ps", tag="ctx_ps")
+        def is_round(r):
+            return 0 <= r < N_ROUNDS
+
+        def place(r, i):
+            blk, part = divmod(r, ROUNDS_PER_BLOCK)
+            return blk, part * R + i
+
+        def transpose_head(r, i, h):
+            blk, j = place(r, i)
+            g, t = divmod(h, PACK)
+            nc.tensor.transpose(
+                qT_ps[r][i][:, h, :], q_tiles[blk * PASSES + g][:, t, j * DH : (j + 1) * DH], identity[:]
+            )
+
+        def multiply_head(r, i, h):
+            g, t = divmod(h, PACK)
+            b = place(r, i)[0] // BLOCKS_PER_SEQ
             nc.tensor.matmul(
-                out=ctx_ps[u, t][:],
-                lhsT=kv_sb[:, blk // BLOCKS_PER_SEQ, g * PACK + t, :],
-                rhs=qT_sb[u][:, t, :],
+                out=ctx_ps[r][i][g][:, t, :],
+                lhsT=kv_sb[:, b, h, :],
+                rhs=qT_sb[r][:, i, h, :],
                 start=True,
                 stop=True,
             )
 
-        def transpose_unit(u):
-            qT_ps[u] = [
-                qT_banks.tile([P, HEADS_PER_BANK, BLOCK], BF16, name="qT_ps", tag="qT_ps")
-                for bank in range(PACK // HEADS_PER_BANK)
-            ]
-            for t in range(PACK):
-                for j in range(J):
-                    nc.tensor.transpose(
-                        qT_ps[u][t // HEADS_PER_BANK][:, t % HEADS_PER_BANK, j * P : (j + 1) * P],
-                        q_tiles[u][:, t, j * DH : (j + 1) * DH],
-                        identity[:],
-                    )
+        def transposes_and_plain_matmuls(r_t, r_m):
+            if is_round(r_t):
+                qT_ps[r_t] = [qT_banks.tile([P, H, P], BF16, name="qT_ps", tag="qT_ps") for i in range(R)]
+            if is_round(r_m):
+                ctx_ps[r_m] = [
+                    [ctx_banks.tile([P, PACK, P], F32, name="ctx_ps", tag="ctx_ps") for g in range(PASSES)]
+                    for i in range(R)
+                ]
+            for i in range(R):
+                for h in range(0, H, 2):
+                    if is_round(r_m):
+                        multiply_head(r_m, i, h)
+                    if is_round(r_t):
+                        transpose_head(r_t, i, h)
+                        transpose_head(r_t, i, h + 1)
+                    if is_round(r_m):
+                        multiply_head(r_m, i, h + 1)
 
-        def transposes_and_plain_matmuls(u_t, u_m):
-            if is_unit(u_m):
-                plain_matmul(u_m, 0)
-                plain_matmul(u_m, 1)
-            if is_unit(u_t):
-                transpose_unit(u_t)
-            if is_unit(u_m):
-                plain_matmul(u_m, 2)
-                plain_matmul(u_m, 3)
+        def copy_transposed(r):
+            if is_round(r):
+                qT_sb[r] = work.tile([P, R, H, P], BF16, name="qT_sb", tag="qT_sb")
+                for i in range(R):
+                    nc.scalar.copy(out=qT_sb[r][:, i], in_=qT_ps[r][i][:])
 
-        def heads_on_vector(u):
-            return 2 if u == 0 else u % 2
-
-        def divide_head(u, t):
-            blk, g = divmod(u, PASSES)
-            head = (blk // BLOCKS_PER_SEQ) * H + g * PACK + t
-            if t >= PACK - heads_on_vector(u):
-                nc.vector.tensor_scalar_mul(out=ctx_sb[u][:, t, :], in0=ctx_ps[u, t][:], scalar1=rden[:, head : head + 1])
-            else:
-                nc.scalar.activation(
-                    out=ctx_sb[u][:, t, :],
-                    in_=ctx_ps[u, t][:],
-                    func=mybir.ActivationFunctionType.Copy,
-                    scale=rden[:, head : head + 1],
-                )
-
-        def leave_psum(u_t, u_m):
-            if is_unit(u_m):
-                ctx_sb[u_m] = work.tile([P, PACK, BLOCK], BF16, name="ctx_sb", tag="ctx_sb")
-                divide_head(u_m, 0)
-                divide_head(u_m, 1)
-            if is_unit(u_t):
-                qT_sb[u_t] = work.tile([P, PACK, BLOCK], BF16, name="qT_sb", tag="qT_sb")
-                for bank in range(PACK // HEADS_PER_BANK):
-                    heads = slice(bank * HEADS_PER_BANK, (bank + 1) * HEADS_PER_BANK)
-                    nc.scalar.copy(out=qT_sb[u_t][:, heads, :], in_=qT_ps[u_t][bank][:])
-            if is_unit(u_m):
-                divide_head(u_m, 2)
-                divide_head(u_m, 3)
-
-        def regroup(u):
-            if is_unit(u):
-                grouped[u] = work.tile([P, BLOCK, PACK], BF16, name="grouped", tag="grouped", align_bytes=64)
-                side_by_side(grouped[u][:], ctx_sb[u][:])
-
-        def quantise(u):
-            if is_unit(u):
-                codes[u] = mx_pool.tile([P, BLOCK], U32, name="codes", tag="codes", align_bytes=64)
-                scales[u] = mx_pool.tile([P, BLOCK], U8, name="scales", tag="scales", align_bytes=64)
-                nc.vector.quantize_mx(
-                    out=codes[u][:].bitcast(FP8X4),
-                    scales=scales[u][:],
-                    in_=grouped[u][:].rearrange("p s t -> p (s t)"),
-                )
-
-        def project(pair):
-            blk, second = divmod(pair, J // PAIR)
-            out_ps[pair] = [out_banks.tile([P, E], F32, name="out_ps", tag="out_ps") for i in range(PAIR)]
-            for i in range(PAIR):
-                cols = slice((second * PAIR + i) * P, (second * PAIR + i + 1) * P)
+        def divide_tile(r, i):
+            if is_round(r):
+                if i == 0:
+                    grouped[r] = work.tile([P, R, PASSES, P, PACK], BF16, name="grouped", tag="grouped", align_bytes=64)
+                b = place(r, i)[0] // BLOCKS_PER_SEQ
                 for g in range(PASSES):
-                    nc.tensor.matmul_mx(
-                        out=out_ps[pair][i][:],
-                        lhsT=codes[blk * PASSES + g][:, cols].bitcast(FP8X4),
-                        lhsT_scale=scales[blk * PASSES + g][:, cols],
-                        rhs=wo_codes[:, g, :].bitcast(FP8X4),
-                        rhs_scale=wo_scales[:, g, :],
-                        start=(g == 0),
-                        stop=(g == PASSES - 1),
+                    first = b * H + g * PACK
+                    nc.vector.tensor_tensor(
+                        out=grouped[r][:, i, g],
+                        in0=ctx_ps[r][i][g][:].rearrange("p t s -> p s t"),
+                        in1=rden[:, first : first + PACK].unsqueeze(1).to_broadcast([P, P, PACK]),
+                        op=mybir.AluOpType.mult,
                     )
 
-        def add_bias_and_store(pair, i):
-            nc.vector.tensor_tensor(
-                out=out_sb[pair][:, i, :], in0=out_ps[pair][i][:], in1=bias_sb[:], op=mybir.AluOpType.add
-            )
-            blk, second = divmod(pair, J // PAIR)
-            b, part = divmod(blk, BLOCKS_PER_SEQ)
-            rows = out[b, part * BLOCK : (part + 1) * BLOCK, :].rearrange("(p j) n -> p j n", j=J)
-            nc.sync.dma_start(out=rows[:, second * PAIR + i, :], in_=out_sb[pair][:, i, :])
+        def quantise(r):
+            if is_round(r):
+                codes[r] = mx_pool.tile([P, R, PASSES, P], U32, name="codes", tag="codes", align_bytes=64)
+                scales[r] = mx_pool.tile([P, R, PASSES, P], U8, name="scales", tag="scales", align_bytes=64)
+                nc.vector.quantize_mx(
+                    out=codes[r][:].rearrange("p i g s -> p (i g s)").bitcast(FP8X4),
+                    scales=scales[r][:].rearrange("p i g s -> p (i g s)"),
+                    in_=grouped[r][:].rearrange("p i g s t -> p (i g s t)"),
+                )
 
-        def pipeline_step(step):
-            transposes_and_plain_matmuls(step, step - 1)
-            pair = step - PROJECT_LAG
-            if 0 <= pair < N_PAIRS:
-                project(pair)
-                out_sb[pair] = out_pool.tile([P, PAIR, E], F32, name="out_sb", tag="out_sb")
-                add_bias_and_store(pair, 0)
-            quantise(step - 2)
-            if 0 <= pair < N_PAIRS:
-                add_bias_and_store(pair, 1)
-                if is_unit(pair + LOADS_AHEAD):
-                    load_unit(pair + LOADS_AHEAD)
-            leave_psum(step, step - 1)
-            regroup(step - 1)
+        def project(r):
+            if is_round(r):
+                out_ps[r] = [out_banks.tile([P, E], F32, name="out_ps", tag="out_ps") for i in range(R)]
+                for i in range(R):
+                    for g in range(PASSES):
+                        nc.tensor.matmul_mx(
+                            out=out_ps[r][i][:],
+                            lhsT=codes[r][:, i, g, :].bitcast(FP8X4),
+                            lhsT_scale=scales[r][:, i, g, :],
+                            rhs=wo_codes[:, g, :].bitcast(FP8X4),
+                            rhs_scale=wo_scales[:, g, :],
+                            start=(g == 0),
+                            stop=(g == PASSES - 1),
+                        )
 
-        for step in range(N_PAIRS + PROJECT_LAG):
-            pipeline_step(step)
-            if step == 0:
+        def add_bias_and_store(r, vector_is_free):
+            if is_round(r):
+                out_sb[r] = out_pool.tile([P, R, E], F32, name="out_sb", tag="out_sb")
+                for i in range(R):
+                    if vector_is_free:
+                        nc.vector.tensor_tensor(
+                            out=out_sb[r][:, i, :], in0=out_ps[r][i][:], in1=bias_sb[:], op=mybir.AluOpType.add
+                        )
+                    else:
+                        nc.scalar.copy(out=out_sb[r][:, i, :], in_=out_ps[r][i][:])
+                        nc.gpsimd.tensor_tensor(
+                            out=out_sb[r][:, i, :], in0=out_sb[r][:, i, :], in1=bias_sb[:], op=mybir.AluOpType.add
+                        )
+                    blk, j = place(r, i)
+                    b, part = divmod(blk, BLOCKS_PER_SEQ)
+                    rows = out[b, part * BLOCK : (part + 1) * BLOCK, :].rearrange("(p j) n -> p j n", j=J)
+                    nc.sync.dma_start(out=rows[:, j, :], in_=out_sb[r][:, i, :])
+                if r + LOADS_AHEAD < N_LOADS:
+                    load_q(r + LOADS_AHEAD)
+
+        for k in range(N_ROUNDS + 3):
+            transposes_and_plain_matmuls(k, k - 1)
+            copy_transposed(k)
+            if k == 0:
                 nc.vector.reciprocal(out=rden[:], in_=denom_bc[:])
-            if step == PROJECT_LAG - 2:
-                prepare_projection()
+                spread_bias()
+            if 1 <= k < 1 + PASSES:
+                regroup_wo(k - 1)
+            divide_tile(k - 1, 0)
+            quantise(k - 2)
+            divide_tile(k - 1, 1)
+            if 2 <= k < 2 + PASSES:
+                quantise_wo(k - 2)
+            project(k - 3)
+            add_bias_and_store(k - 3, vector_is_free=not is_round(k - 1))

from contextlib import ExitStack

import concourse.masks as masks
import concourse.mybir as mybir

BF16 = mybir.dt.bfloat16
F32 = mybir.dt.float32
U32 = mybir.dt.uint32
U8 = mybir.dt.uint8
FP8X4 = mybir.dt.float8_e4m3fn_x4

P = 128
B, H, S, DH, E = 2, 8, 4096, 128, 512
PACK = 4
PASSES = H // PACK
J = 4
BLOCK = P * J
BLOCKS_PER_SEQ = S // BLOCK
N_LOADS = B * BLOCKS_PER_SEQ * PASSES
R = 2
ROUNDS_PER_BLOCK = J // R
N_ROUNDS = B * S // (R * P)
LOADS_AHEAD = 8

FLOPS = 2 * B * H * S * DH * DH + 2 * B * S * H * DH * E


def tile_linearattention_pb_t_kernel(tc, q_feat, kv, denom, Wo, bo, out):
    nc = tc.nc
    with ExitStack() as stack:
        const = stack.enter_context(tc.tile_pool(name="const", bufs=1))
        q_pool = stack.enter_context(tc.tile_pool(name="q", bufs=LOADS_AHEAD + 4))
        work = stack.enter_context(tc.tile_pool(name="work", bufs=2))
        mx_pool = stack.enter_context(tc.tile_pool(name="mx", bufs=3))
        out_pool = stack.enter_context(tc.tile_pool(name="outs", bufs=4))
        qT_banks = stack.enter_context(tc.psum_pool(name="qT_banks", bufs=R))
        ctx_banks = stack.enter_context(tc.psum_pool(name="ctx_banks", bufs=R * PASSES))
        out_banks = stack.enter_context(tc.psum_pool(name="out_banks", bufs=R))
        stack.enter_context(tc.manual_schedule())

        q_tiles = {}

        def load_q(n):
            blk, g = divmod(n, PASSES)
            b, part = divmod(blk, BLOCKS_PER_SEQ)
            q_tiles[n] = q_pool.tile([P, PACK, J * DH], BF16, name="q_sb", tag="q_sb")
            rows = q_feat[b, g * PACK : (g + 1) * PACK, part * BLOCK : (part + 1) * BLOCK, :]
            nc.sync.dma_start(out=q_tiles[n][:], in_=rows.rearrange("h (p j) d -> p h (j d)", j=J))

        bias_row = const.tile([P, E], BF16)
        nc.vector.memset(bias_row[:], 0.0)
        ones = const.tile([P, P], BF16)
        nc.vector.memset(ones[:], 1.0)
        identity = const.tile([P, P], BF16)
        masks.make_identity(nc, identity[:])

        load_q(0)
        load_q(1)
        kv_sb = const.tile([P, B, H, DH], BF16)
        nc.sync.dma_start(out=kv_sb[:, 0], in_=kv[0].rearrange("h d e -> d h e"))
        denom_bc = const.tile([P, B * H], BF16)
        nc.sync.dma_start(out=denom_bc[:], in_=denom.rearrange("b h x y -> (b h x y)").partition_broadcast(P))
        nc.sync.dma_start(out=bias_row[0:1, :], in_=bo.rearrange("(o n) -> o n", o=1))
        wo_raw = const.tile([P, H, E], BF16)
        nc.sync.dma_start(out=wo_raw[:], in_=Wo.rearrange("(c p) n -> p c n", p=P))
        for n in range(2, LOADS_AHEAD):
            load_q(n)
        nc.sync.dma_start(out=kv_sb[:, 1], in_=kv[1].rearrange("h d e -> d h e"))

        rden = const.tile([P, B * H], F32)
        bias_sb = const.tile([P, E], F32)
        wo_grouped = const.tile([P, PASSES, E, PACK], BF16, align_bytes=64)
        wo_codes = const.tile([P, PASSES, E], U32, align_bytes=64)
        wo_scales = const.tile([P, PASSES, E], U8, align_bytes=64)

        def spread_bias():
            bias_ps = out_banks.tile([P, E], F32, name="bias_ps", tag="out_ps")
            nc.tensor.matmul(out=bias_ps[:], lhsT=ones[:], rhs=bias_row[:], start=True, stop=True)
            nc.scalar.copy(out=bias_sb[:], in_=bias_ps[:])

        def regroup_wo(g):
            nc.scalar.copy(
                out=wo_grouped[:, g].rearrange("p (c i) t -> p c t i", i=4),
                in_=wo_raw[:, g * PACK : (g + 1) * PACK, :].rearrange("p t (c i) -> p c t i", i=4),
            )

        def quantise_wo(g):
            nc.vector.quantize_mx(
                out=wo_codes[:, g, :].bitcast(FP8X4),
                scales=wo_scales[:, g, :],
                in_=wo_grouped[:, g].rearrange("p n t -> p (n t)"),
            )

        qT_ps, qT_sb, ctx_ps, grouped, codes, scales, out_ps, out_sb = {}, {}, {}, {}, {}, {}, {}, {}

        def is_round(r):
            return 0 <= r < N_ROUNDS

        def place(r, i):
            blk, part = divmod(r, ROUNDS_PER_BLOCK)
            return blk, part * R + i

        def transpose_head(r, i, h):
            blk, j = place(r, i)
            g, t = divmod(h, PACK)
            nc.tensor.transpose(
                qT_ps[r][i][:, h, :], q_tiles[blk * PASSES + g][:, t, j * DH : (j + 1) * DH], identity[:]
            )

        def multiply_head(r, i, h):
            g, t = divmod(h, PACK)
            b = place(r, i)[0] // BLOCKS_PER_SEQ
            nc.tensor.matmul(
                out=ctx_ps[r][i][g][:, t, :],
                lhsT=kv_sb[:, b, h, :],
                rhs=qT_sb[r][:, i, h, :],
                start=True,
                stop=True,
            )

        def transposes_and_plain_matmuls(r_t, r_m):
            if is_round(r_t):
                qT_ps[r_t] = [qT_banks.tile([P, H, P], BF16, name="qT_ps", tag="qT_ps") for i in range(R)]
            if is_round(r_m):
                ctx_ps[r_m] = [
                    [ctx_banks.tile([P, PACK, P], F32, name="ctx_ps", tag="ctx_ps") for g in range(PASSES)]
                    for i in range(R)
                ]
            for i in range(R):
                for h in range(0, H, 2):
                    if is_round(r_m):
                        multiply_head(r_m, i, h)
                    if is_round(r_t):
                        transpose_head(r_t, i, h)
                        transpose_head(r_t, i, h + 1)
                    if is_round(r_m):
                        multiply_head(r_m, i, h + 1)

        def copy_transposed(r):
            if is_round(r):
                qT_sb[r] = work.tile([P, R, H, P], BF16, name="qT_sb", tag="qT_sb")
                for i in range(R):
                    nc.scalar.copy(out=qT_sb[r][:, i], in_=qT_ps[r][i][:])

        def divide_tile(r, i):
            if is_round(r):
                if i == 0:
                    grouped[r] = work.tile([P, R, PASSES, P, PACK], BF16, name="grouped", tag="grouped", align_bytes=64)
                b = place(r, i)[0] // BLOCKS_PER_SEQ
                for g in range(PASSES):
                    first = b * H + g * PACK
                    nc.vector.tensor_tensor(
                        out=grouped[r][:, i, g],
                        in0=ctx_ps[r][i][g][:].rearrange("p t s -> p s t"),
                        in1=rden[:, first : first + PACK].unsqueeze(1).to_broadcast([P, P, PACK]),
                        op=mybir.AluOpType.mult,
                    )

        def quantise(r):
            if is_round(r):
                codes[r] = mx_pool.tile([P, R, PASSES, P], U32, name="codes", tag="codes", align_bytes=64)
                scales[r] = mx_pool.tile([P, R, PASSES, P], U8, name="scales", tag="scales", align_bytes=64)
                nc.vector.quantize_mx(
                    out=codes[r][:].rearrange("p i g s -> p (i g s)").bitcast(FP8X4),
                    scales=scales[r][:].rearrange("p i g s -> p (i g s)"),
                    in_=grouped[r][:].rearrange("p i g s t -> p (i g s t)"),
                )

        def project(r):
            if is_round(r):
                out_ps[r] = [out_banks.tile([P, E], F32, name="out_ps", tag="out_ps") for i in range(R)]
                for i in range(R):
                    for g in range(PASSES):
                        nc.tensor.matmul_mx(
                            out=out_ps[r][i][:],
                            lhsT=codes[r][:, i, g, :].bitcast(FP8X4),
                            lhsT_scale=scales[r][:, i, g, :],
                            rhs=wo_codes[:, g, :].bitcast(FP8X4),
                            rhs_scale=wo_scales[:, g, :],
                            start=(g == 0),
                            stop=(g == PASSES - 1),
                        )

        def add_bias_and_store(r, vector_is_free):
            if is_round(r):
                out_sb[r] = out_pool.tile([P, R, E], F32, name="out_sb", tag="out_sb")
                for i in range(R):
                    if vector_is_free:
                        nc.vector.tensor_tensor(
                            out=out_sb[r][:, i, :], in0=out_ps[r][i][:], in1=bias_sb[:], op=mybir.AluOpType.add
                        )
                    else:
                        nc.scalar.copy(out=out_sb[r][:, i, :], in_=out_ps[r][i][:])
                        nc.gpsimd.tensor_tensor(
                            out=out_sb[r][:, i, :], in0=out_sb[r][:, i, :], in1=bias_sb[:], op=mybir.AluOpType.add
                        )
                    blk, j = place(r, i)
                    b, part = divmod(blk, BLOCKS_PER_SEQ)
                    rows = out[b, part * BLOCK : (part + 1) * BLOCK, :].rearrange("(p j) n -> p j n", j=J)
                    nc.sync.dma_start(out=rows[:, j, :], in_=out_sb[r][:, i, :])
                if r + LOADS_AHEAD < N_LOADS:
                    load_q(r + LOADS_AHEAD)

        for k in range(N_ROUNDS + 3):
            transposes_and_plain_matmuls(k, k - 1)
            copy_transposed(k)
            if k == 0:
                nc.vector.reciprocal(out=rden[:], in_=denom_bc[:])
                spread_bias()
            if 1 <= k < 1 + PASSES:
                regroup_wo(k - 1)
            divide_tile(k - 1, 0)
            quantise(k - 2)
            divide_tile(k - 1, 1)
            if 2 <= k < 2 + PASSES:
                quantise_wo(k - 2)
            project(k - 3)
            add_bias_and_store(k - 3, vector_is_free=not is_round(k - 1))
